import numpy as np
import ml_dtypes

BF16 = ml_dtypes.bfloat16


def bf(x):
    return np.asarray(x, np.float32).astype(BF16)


def f32(x):
    return np.asarray(x, np.float32)


def f64(x):
    return np.asarray(x).astype(np.float64)


def striped(idx):
    return np.tile(idx.reshape(-1, 16).T, (8, 1))


T, CI, CO, K, S, N = 4, 128, 128, 2, 512, 256
EDGE_PROB = 0.02


def setup_inputs():
    a = (np.random.random((N, N)) < EDGE_PROB).astype(np.float32)
    a = np.maximum(np.maximum(a, a.T), np.eye(N, dtype=np.float32))
    return {"x": f32(bf(np.random.standard_normal((T * CI, S)))), "adj": bf(a), "w": bf(np.random.standard_normal((K * CI, CO)) / np.sqrt(K * CI)), "b": f32(0.1 * np.random.standard_normal((CO, 1))), "offs": striped(np.random.permutation(S)[:N])}


def reference(x, adj, w, b, offs):
    idx = offs[:16].T.reshape(-1)
    h = f64(x)[:, idx].reshape(T, CI, N)
    a = f64(adj)
    dis = 1.0 / np.sqrt(a.sum(axis=1))
    tx1 = h - ((h * dis) @ a.T) * dis
    cat = np.concatenate([h, tx1], axis=1)
    return (f64(w).T @ cat + f64(b)).reshape(T * CO, N)

@@ -1,0 +1,81 @@
+import concourse.mybir as mybir
+from concourse.masks import make_identity
+
+F32, BF16, U16 = mybir.dt.float32, mybir.dt.bfloat16, mybir.dt.uint16
+ACT = mybir.ActivationFunctionType
+ALU = mybir.AluOpType
+
+P = 128
+T = 4
+S = 512
+N = 256
+NB = N // P
+
+FLOPS = T * (2 * P * N * N + 2 * (2 * P) * P * N)
+BYTES = 4 * T * P * N + 2 * N * N + 2 * 2 * P * P + 4 * P + 2 * P * (N // 16) + 4 * T * P * N
+
+
+def tile_adaptivegraphconv_kernel(tc, x, adj, w, b, offs, out):
+    nc = tc.nc
+    with (
+        tc.tile_pool(name="held", bufs=1) as held,
+        tc.tile_pool(name="step", bufs=T) as step,
+        tc.psum_pool(name="psum_once", bufs=1) as psum_once,
+        tc.psum_pool(name="psum", bufs=2) as psum,
+    ):
+        offsets = held.tile([P, N // 16], U16, name="offsets")
+        nc.sync.dma_start(offsets[:], offs)
+        adj_sb = held.tile([P, NB, N], BF16, name="adj_sb")
+        nc.scalar.dma_start(adj_sb[:], adj.rearrange("(nb p) j -> p nb j", p=P))
+        w_sb = held.tile([P, 2, P], BF16, name="w_sb")
+        nc.scalar.dma_start(w_sb[:], w.rearrange("(k c) o -> c k o", c=P))
+        bias = held.tile([P, 1], F32, name="bias")
+        nc.scalar.dma_start(bias[:], b)
+        windows = [held.tile([P, S], F32, name=f"window{t}") for t in range(T)]
+        for t in range(T):
+            nc.sync.dma_start(windows[t][:], x[t * P : (t + 1) * P, :])
+
+        identity = held.tile([P, P], F32, name="identity")
+        make_identity(nc, identity[:])
+        ones = held.tile([P, P], BF16, name="ones")
+        nc.vector.memset(ones[:], 1.0)
+
+        deg_col = held.tile([P, NB], F32, name="deg_col")
+        nc.vector.tensor_reduce(deg_col[:], adj_sb[:], axis=mybir.AxisListType.X, op=ALU.add)
+        deg_row_ps = psum_once.tile([P, N], F32, name="deg_row_ps")
+        for nb in range(NB):
+            nc.tensor.matmul(deg_row_ps[:], ones[:], adj_sb[:, nb, :], start=(nb == 0), stop=(nb == NB - 1))
+        dis_col = held.tile([P, NB], F32, name="dis_col")
+        nc.scalar.activation(dis_col[:], deg_col[:], ACT.Abs_reciprocal_sqrt)
+        dis_row = held.tile([P, N], F32, name="dis_row")
+        nc.scalar.activation(dis_row[:], deg_row_ps[:], ACT.Abs_reciprocal_sqrt)
+        adj_hat = held.tile([P, NB, N], BF16, name="adj_hat")
+        for nb in range(NB):
+            nc.vector.scalar_tensor_tensor(
+                adj_hat[:, nb, :], adj_sb[:, nb, :], dis_col[:, nb : nb + 1], dis_row[:], op0=ALU.mult, op1=ALU.mult
+            )
+
+        for t in range(T):
+            h = step.tile([P, N], F32, name="h")
+            nc.scalar.activation(h[:], windows[t][:].indirect(offsets[:]), ACT.Copy)
+            h_bf = step.tile([P, N], BF16, name="h_bf")
+            nc.gpsimd.tensor_copy(h_bf[:], h[:])
+
+            hT_ps = psum.tile([P, NB, P], F32, name="hT_ps")
+            for nb in range(NB):
+                nc.tensor.transpose(hT_ps[:, nb, :], h[:, nb * P : (nb + 1) * P], identity[:])
+            hT = step.tile([P, NB, P], BF16, name="hT")
+            nc.vector.tensor_copy(hT[:], hT_ps[:])
+
+            prop_ps = psum.tile([P, N], F32, name="prop_ps")
+            for nb in range(NB):
+                nc.tensor.matmul(prop_ps[:], hT[:, nb, :], adj_hat[:, nb, :], start=(nb == 0), stop=(nb == NB - 1))
+            tx1 = step.tile([P, N], BF16, name="tx1")
+            nc.vector.tensor_tensor(tx1[:], h[:], prop_ps[:], ALU.subtract)
+
+            out_ps = psum.tile([P, N], F32, name="out_ps")
+            nc.tensor.matmul(out_ps[:], w_sb[:, 0, :], h_bf[:], start=True, stop=False)
+            nc.tensor.matmul(out_ps[:], w_sb[:, 1, :], tx1[:], start=False, stop=True)
+            out_sb = step.tile([P, N], F32, name="out_sb")
+            nc.scalar.activation(out_sb[:], out_ps[:], ACT.Identity, bias=bias[:])
+            nc.sync.dma_start(out[t * P : (t + 1) * P, :], out_sb[:])

@@ -1,5 +1,4 @@
 import concourse.mybir as mybir
-from concourse.masks import make_identity
 
 F32, BF16, U16 = mybir.dt.float32, mybir.dt.bfloat16, mybir.dt.uint16
 ACT = mybir.ActivationFunctionType
@@ -20,8 +19,7 @@ def tile_adaptivegraphconv_kernel(tc, x, adj, w, b, offs, out):
     with (
         tc.tile_pool(name="held", bufs=1) as held,
         tc.tile_pool(name="step", bufs=T) as step,
-        tc.psum_pool(name="psum_once", bufs=1) as psum_once,
-        tc.psum_pool(name="psum", bufs=2) as psum,
+        tc.psum_pool(name="psum", bufs=T) as psum,
     ):
         offsets = held.tile([P, N // 16], U16, name="offsets")
         nc.sync.dma_start(offsets[:], offs)
@@ -35,14 +33,14 @@ def tile_adaptivegraphconv_kernel(tc, x, adj, w, b, offs, out):
         for t in range(T):
             nc.sync.dma_start(windows[t][:], x[t * P : (t + 1) * P, :])
 
-        identity = held.tile([P, P], F32, name="identity")
-        make_identity(nc, identity[:])
         ones = held.tile([P, P], BF16, name="ones")
         nc.vector.memset(ones[:], 1.0)
+        w1_neg = held.tile([P, P], BF16, name="w1_neg")
+        nc.vector.tensor_scalar_mul(w1_neg[:], w_sb[:, 1, :], -1.0)
 
         deg_col = held.tile([P, NB], F32, name="deg_col")
         nc.vector.tensor_reduce(deg_col[:], adj_sb[:], axis=mybir.AxisListType.X, op=ALU.add)
-        deg_row_ps = psum_once.tile([P, N], F32, name="deg_row_ps")
+        deg_row_ps = psum.tile([P, N], F32, name="deg_row_ps", tag="mixed_ps")
         for nb in range(NB):
             nc.tensor.matmul(deg_row_ps[:], ones[:], adj_sb[:, nb, :], start=(nb == 0), stop=(nb == NB - 1))
         dis_col = held.tile([P, NB], F32, name="dis_col")
@@ -59,23 +57,19 @@ def tile_adaptivegraphconv_kernel(tc, x, adj, w, b, offs, out):
             h = step.tile([P, N], F32, name="h")
             nc.scalar.activation(h[:], windows[t][:].indirect(offsets[:]), ACT.Copy)
             h_bf = step.tile([P, N], BF16, name="h_bf")
-            nc.gpsimd.tensor_copy(h_bf[:], h[:])
+            nc.vector.tensor_copy(h_bf[:], h[:])
 
-            hT_ps = psum.tile([P, NB, P], F32, name="hT_ps")
+            mixed_ps = psum.tile([P, NB, P], F32, name="mixed_ps")
             for nb in range(NB):
-                nc.tensor.transpose(hT_ps[:, nb, :], h[:, nb * P : (nb + 1) * P], identity[:])
-            hT = step.tile([P, NB, P], BF16, name="hT")
-            nc.vector.tensor_copy(hT[:], hT_ps[:])
-
-            prop_ps = psum.tile([P, N], F32, name="prop_ps")
-            for nb in range(NB):
-                nc.tensor.matmul(prop_ps[:], hT[:, nb, :], adj_hat[:, nb, :], start=(nb == 0), stop=(nb == NB - 1))
-            tx1 = step.tile([P, N], BF16, name="tx1")
-            nc.vector.tensor_tensor(tx1[:], h[:], prop_ps[:], ALU.subtract)
+                nc.tensor.matmul(mixed_ps[:, nb, :], h_bf[:, nb * P : (nb + 1) * P], w1_neg[:], start=True, stop=True)
+            mixed = step.tile([P, NB, P], BF16, name="mixed")
+            nc.vector.tensor_copy(mixed[:], mixed_ps[:])
 
             out_ps = psum.tile([P, N], F32, name="out_ps")
             nc.tensor.matmul(out_ps[:], w_sb[:, 0, :], h_bf[:], start=True, stop=False)
-            nc.tensor.matmul(out_ps[:], w_sb[:, 1, :], tx1[:], start=False, stop=True)
+            nc.tensor.matmul(out_ps[:], w_sb[:, 1, :], h_bf[:], start=False, stop=False)
+            for nb in range(NB):
+                nc.tensor.matmul(out_ps[:], mixed[:, nb, :], adj_hat[:, nb, :], start=False, stop=(nb == NB - 1))
             out_sb = step.tile([P, N], F32, name="out_sb")
             nc.scalar.activation(out_sb[:], out_ps[:], ACT.Identity, bias=bias[:])
             nc.sync.dma_start(out[t * P : (t + 1) * P, :], out_sb[:])

@@ -56,8 +56,7 @@ def tile_adaptivegraphconv_kernel(tc, x, adj, w, b, offs, out):
         for t in range(T):
             h = step.tile([P, N], F32, name="h")
             nc.scalar.activation(h[:], windows[t][:].indirect(offsets[:]), ACT.Copy)
-            h_bf = step.tile([P, N], BF16, name="h_bf")
-            nc.vector.tensor_copy(h_bf[:], h[:])
+            h_bf = h[:].bitcast(BF16).rearrange("c (j half) -> c j half", half=2)[:, :, 1]
 
             mixed_ps = psum.tile([P, NB, P], F32, name="mixed_ps")
             for nb in range(NB):
@@ -66,8 +65,8 @@ def tile_adaptivegraphconv_kernel(tc, x, adj, w, b, offs, out):
             nc.vector.tensor_copy(mixed[:], mixed_ps[:])
 
             out_ps = psum.tile([P, N], F32, name="out_ps")
-            nc.tensor.matmul(out_ps[:], w_sb[:, 0, :], h_bf[:], start=True, stop=False)
-            nc.tensor.matmul(out_ps[:], w_sb[:, 1, :], h_bf[:], start=False, stop=False)
+            nc.tensor.matmul(out_ps[:], w_sb[:, 0, :], h_bf, start=True, stop=False)
+            nc.tensor.matmul(out_ps[:], w_sb[:, 1, :], h_bf, start=False, stop=False)
             for nb in range(NB):
                 nc.tensor.matmul(out_ps[:], mixed[:, nb, :], adj_hat[:, nb, :], start=False, stop=(nb == NB - 1))
             out_sb = step.tile([P, N], F32, name="out_sb")

@@ -9,6 +9,7 @@ T = 4
 S = 512
 N = 256
 NB = N // P
+WARM = 12
 
 FLOPS = T * (2 * P * N * N + 2 * (2 * P) * P * N)
 BYTES = 4 * T * P * N + 2 * N * N + 2 * 2 * P * P + 4 * P + 2 * P * (N // 16) + 4 * T * P * N
@@ -35,6 +36,10 @@ def tile_adaptivegraphconv_kernel(tc, x, adj, w, b, offs, out):
 
         ones = held.tile([P, P], BF16, name="ones")
         nc.vector.memset(ones[:], 1.0)
+        warm_ps = psum.tile([P, P], F32, name="warm_ps", tag="out_ps")
+        for i in range(WARM):
+            nc.tensor.matmul(warm_ps[:], ones[:], ones[:], start=True, stop=True)
+
         w1_neg = held.tile([P, P], BF16, name="w1_neg")
         nc.vector.tensor_scalar_mul(w1_neg[:], w_sb[:, 1, :], -1.0)
 

@@ -63,7 +63,7 @@ def tile_adaptivegraphconv_kernel(tc, x, adj, w, b, offs, out):
             nc.scalar.activation(h[:], windows[t][:].indirect(offsets[:]), ACT.Copy)
             h_bf = h[:].bitcast(BF16).rearrange("c (j half) -> c j half", half=2)[:, :, 1]
 
-            mixed_ps = psum.tile([P, NB, P], F32, name="mixed_ps")
+            mixed_ps = psum.tile([P, NB, P], BF16, name="mixed_ps")
             for nb in range(NB):
                 nc.tensor.matmul(mixed_ps[:, nb, :], h_bf[:, nb * P : (nb + 1) * P], w1_neg[:], start=True, stop=True)
             mixed = step.tile([P, NB, P], BF16, name="mixed")

@@ -58,22 +58,32 @@ def tile_adaptivegraphconv_kernel(tc, x, adj, w, b, offs, out):
                 adj_hat[:, nb, :], adj_sb[:, nb, :], dis_col[:, nb : nb + 1], dis_row[:], op0=ALU.mult, op1=ALU.mult
             )
 
-        for t in range(T):
-            h = step.tile([P, N], F32, name="h")
-            nc.scalar.activation(h[:], windows[t][:].indirect(offsets[:]), ACT.Copy)
-            h_bf = h[:].bitcast(BF16).rearrange("c (j half) -> c j half", half=2)[:, :, 1]
+        mixeds, out_pss = [], []
+        for u in range(T + 1):
+            if u < T:
+                t = u
+                h = step.tile([P, N], F32, name="h")
+                nc.scalar.activation(h[:], windows[t][:].indirect(offsets[:]), ACT.Copy)
+                h_bf = h[:].bitcast(BF16).rearrange("c (j half) -> c j half", half=2)[:, :, 1]
 
-            mixed_ps = psum.tile([P, NB, P], BF16, name="mixed_ps")
-            for nb in range(NB):
-                nc.tensor.matmul(mixed_ps[:, nb, :], h_bf[:, nb * P : (nb + 1) * P], w1_neg[:], start=True, stop=True)
-            mixed = step.tile([P, NB, P], BF16, name="mixed")
-            nc.vector.tensor_copy(mixed[:], mixed_ps[:])
-
-            out_ps = psum.tile([P, N], F32, name="out_ps")
-            nc.tensor.matmul(out_ps[:], w_sb[:, 0, :], h_bf, start=True, stop=False)
-            nc.tensor.matmul(out_ps[:], w_sb[:, 1, :], h_bf, start=False, stop=False)
-            for nb in range(NB):
-                nc.tensor.matmul(out_ps[:], mixed[:, nb, :], adj_hat[:, nb, :], start=False, stop=(nb == NB - 1))
-            out_sb = step.tile([P, N], F32, name="out_sb")
-            nc.scalar.activation(out_sb[:], out_ps[:], ACT.Identity, bias=bias[:])
-            nc.sync.dma_start(out[t * P : (t + 1) * P, :], out_sb[:])
+                mixed_ps = psum.tile([P, NB, P], BF16, name="mixed_ps")
+                for nb in range(NB):
+                    nc.tensor.matmul(
+                        mixed_ps[:, nb, :], h_bf[:, nb * P : (nb + 1) * P], w1_neg[:], start=True, stop=True
+                    )
+                mixed = step.tile([P, NB, P], BF16, name="mixed")
+                nc.vector.tensor_copy(mixed[:], mixed_ps[:])
+                out_ps = psum.tile([P, N], F32, name="out_ps")
+                nc.tensor.matmul(out_ps[:], w_sb[:, 0, :], h_bf, start=True, stop=False)
+                nc.tensor.matmul(out_ps[:], w_sb[:, 1, :], h_bf, start=False, stop=False)
+                mixeds.append(mixed)
+                out_pss.append(out_ps)
+            if u >= 1:
+                t = u - 1
+                for nb in range(NB):
+                    nc.tensor.matmul(
+                        out_pss[t][:], mixeds[t][:, nb, :], adj_hat[:, nb, :], start=False, stop=(nb == NB - 1)
+                    )
+                out_sb = step.tile([P, N], F32, name="out_sb")
+                nc.vector.tensor_scalar_add(out_sb[:], out_pss[t][:], bias[:])
+                nc.sync.dma_start(out[t * P : (t + 1) * P, :], out_sb[:])

@@ -21,6 +21,7 @@ def tile_adaptivegraphconv_kernel(tc, x, adj, w, b, offs, out):
         tc.tile_pool(name="held", bufs=1) as held,
         tc.tile_pool(name="step", bufs=T) as step,
         tc.psum_pool(name="psum", bufs=T) as psum,
+        tc.psum_pool(name="psum_mix", bufs=2) as psum_mix,
     ):
         offsets = held.tile([P, N // 16], U16, name="offsets")
         nc.sync.dma_start(offsets[:], offs)
@@ -40,12 +41,14 @@ def tile_adaptivegraphconv_kernel(tc, x, adj, w, b, offs, out):
         for i in range(WARM):
             nc.tensor.matmul(warm_ps[:], ones[:], ones[:], start=True, stop=True)
 
+        w_sum = held.tile([P, P], BF16, name="w_sum")
+        nc.vector.tensor_add(w_sum[:], w_sb[:, 0, :], w_sb[:, 1, :])
         w1_neg = held.tile([P, P], BF16, name="w1_neg")
         nc.vector.tensor_scalar_mul(w1_neg[:], w_sb[:, 1, :], -1.0)
 
         deg_col = held.tile([P, NB], F32, name="deg_col")
         nc.vector.tensor_reduce(deg_col[:], adj_sb[:], axis=mybir.AxisListType.X, op=ALU.add)
-        deg_row_ps = psum.tile([P, N], F32, name="deg_row_ps", tag="mixed_ps")
+        deg_row_ps = psum_mix.tile([P, N], F32, name="deg_row_ps", tag="mixed_ps0")
         for nb in range(NB):
             nc.tensor.matmul(deg_row_ps[:], ones[:], adj_sb[:, nb, :], start=(nb == 0), stop=(nb == NB - 1))
         dis_col = held.tile([P, NB], F32, name="dis_col")
@@ -66,16 +69,13 @@ def tile_adaptivegraphconv_kernel(tc, x, adj, w, b, offs, out):
                 nc.scalar.activation(h[:], windows[t][:].indirect(offsets[:]), ACT.Copy)
                 h_bf = h[:].bitcast(BF16).rearrange("c (j half) -> c j half", half=2)[:, :, 1]
 
-                mixed_ps = psum.tile([P, NB, P], BF16, name="mixed_ps")
-                for nb in range(NB):
-                    nc.tensor.matmul(
-                        mixed_ps[:, nb, :], h_bf[:, nb * P : (nb + 1) * P], w1_neg[:], start=True, stop=True
-                    )
                 mixed = step.tile([P, NB, P], BF16, name="mixed")
-                nc.vector.tensor_copy(mixed[:], mixed_ps[:])
+                for nb in range(NB):
+                    mixed_ps = psum_mix.tile([P, P], BF16, name=f"mixed_ps{nb}")
+                    nc.tensor.matmul(mixed_ps[:], h_bf[:, nb * P : (nb + 1) * P], w1_neg[:], start=True, stop=True)
+                    nc.vector.tensor_copy(mixed[:, nb, :], mixed_ps[:])
                 out_ps = psum.tile([P, N], F32, name="out_ps")
-                nc.tensor.matmul(out_ps[:], w_sb[:, 0, :], h_bf, start=True, stop=False)
-                nc.tensor.matmul(out_ps[:], w_sb[:, 1, :], h_bf, start=False, stop=False)
+                nc.tensor.matmul(out_ps[:], w_sum[:], h_bf, start=True, stop=False)
                 mixeds.append(mixed)
                 out_pss.append(out_ps)
             if u >= 1:

@@ -85,5 +85,7 @@ def tile_adaptivegraphconv_kernel(tc, x, adj, w, b, offs, out):
                         out_pss[t][:], mixeds[t][:, nb, :], adj_hat[:, nb, :], start=False, stop=(nb == NB - 1)
                     )
                 out_sb = step.tile([P, N], F32, name="out_sb")
-                nc.vector.tensor_scalar_add(out_sb[:], out_pss[t][:], bias[:])
-                nc.sync.dma_start(out[t * P : (t + 1) * P, :], out_sb[:])
+                for half in range(2):
+                    cols = slice(half * (N // 2), (half + 1) * (N // 2))
+                    nc.vector.tensor_scalar_add(out_sb[:, cols], out_pss[t][:, cols], bias[:])
+                    nc.sync.dma_start(out[t * P : (t + 1) * P, cols], out_sb[:, cols])

@@ -10,6 +10,7 @@ S = 512
 N = 256
 NB = N // P
 WARM = 12
+WARM_ADJ = 6
 
 FLOPS = T * (2 * P * N * N + 2 * (2 * P) * P * N)
 BYTES = 4 * T * P * N + 2 * N * N + 2 * 2 * P * P + 4 * P + 2 * P * (N // 16) + 4 * T * P * N
@@ -37,9 +38,9 @@ def tile_adaptivegraphconv_kernel(tc, x, adj, w, b, offs, out):
 
         ones = held.tile([P, P], BF16, name="ones")
         nc.vector.memset(ones[:], 1.0)
-        warm_ps = psum.tile([P, P], F32, name="warm_ps", tag="out_ps")
+        warm_ps = psum.tile([P, N], F32, name="warm_ps", tag="out_ps")
         for i in range(WARM):
-            nc.tensor.matmul(warm_ps[:], ones[:], ones[:], start=True, stop=True)
+            nc.tensor.matmul(warm_ps[:, 0:P], ones[:], ones[:], start=True, stop=True)
 
         w_sum = held.tile([P, P], BF16, name="w_sum")
         nc.vector.tensor_add(w_sum[:], w_sb[:, 0, :], w_sb[:, 1, :])
@@ -51,6 +52,8 @@ def tile_adaptivegraphconv_kernel(tc, x, adj, w, b, offs, out):
         deg_row_ps = psum_mix.tile([P, N], F32, name="deg_row_ps", tag="mixed_ps0")
         for nb in range(NB):
             nc.tensor.matmul(deg_row_ps[:], ones[:], adj_sb[:, nb, :], start=(nb == 0), stop=(nb == NB - 1))
+        for i in range(WARM_ADJ):
+            nc.tensor.matmul(warm_ps[:], ones[:], adj_sb[:, i % NB, :], start=True, stop=True)
         dis_col = held.tile([P, NB], F32, name="dis_col")
         nc.scalar.activation(dis_col[:], deg_col[:], ACT.Abs_reciprocal_sqrt)
         dis_row = held.tile([P, N], F32, name="dis_row")

@@ -10,7 +10,7 @@ S = 512
 N = 256
 NB = N // P
 WARM = 12
-WARM_ADJ = 6
+WARM_ADJ = 4
 
 FLOPS = T * (2 * P * N * N + 2 * (2 * P) * P * N)
 BYTES = 4 * T * P * N + 2 * N * N + 2 * 2 * P * P + 4 * P + 2 * P * (N // 16) + 4 * T * P * N

@@ -30,11 +30,11 @@ def tile_adaptivegraphconv_kernel(tc, x, adj, w, b, offs, out):
         nc.scalar.dma_start(adj_sb[:], adj.rearrange("(nb p) j -> p nb j", p=P))
         w_sb = held.tile([P, 2, P], BF16, name="w_sb")
         nc.scalar.dma_start(w_sb[:], w.rearrange("(k c) o -> c k o", c=P))
-        bias = held.tile([P, 1], F32, name="bias")
-        nc.scalar.dma_start(bias[:], b)
         windows = [held.tile([P, S], F32, name=f"window{t}") for t in range(T)]
         for t in range(T):
             nc.sync.dma_start(windows[t][:], x[t * P : (t + 1) * P, :])
+        bias = held.tile([P, 1], F32, name="bias")
+        nc.sync.dma_start(bias[:], b)
 
         ones = held.tile([P, P], BF16, name="ones")
         nc.vector.memset(ones[:], 1.0)

@@ -90,5 +90,9 @@ def tile_adaptivegraphconv_kernel(tc, x, adj, w, b, offs, out):
                 out_sb = step.tile([P, N], F32, name="out_sb")
                 for half in range(2):
                     cols = slice(half * (N // 2), (half + 1) * (N // 2))
-                    nc.vector.tensor_scalar_add(out_sb[:, cols], out_pss[t][:, cols], bias[:])
-                    nc.sync.dma_start(out[t * P : (t + 1) * P, cols], out_sb[:, cols])
+                    if t % 2 == 0:
+                        nc.vector.tensor_scalar_add(out_sb[:, cols], out_pss[t][:, cols], bias[:])
+                        nc.sync.dma_start(out[t * P : (t + 1) * P, cols], out_sb[:, cols])
+                    else:
+                        nc.scalar.activation(out_sb[:, cols], out_pss[t][:, cols], ACT.Identity, bias=bias[:])
+                        nc.scalar.dma_start(out[t * P : (t + 1) * P, cols], out_sb[:, cols])

@@ -24,14 +24,15 @@ def tile_adaptivegraphconv_kernel(tc, x, adj, w, b, offs, out):
         tc.psum_pool(name="psum", bufs=T) as psum,
         tc.psum_pool(name="psum_mix", bufs=2) as psum_mix,
     ):
+        adj_sb = held.tile([P, NB, N], BF16, name="adj_sb")
+        nc.sync.dma_start(adj_sb[:], adj.rearrange("(nb p) j -> p nb j", p=P))
         offsets = held.tile([P, N // 16], U16, name="offsets")
         nc.sync.dma_start(offsets[:], offs)
-        adj_sb = held.tile([P, NB, N], BF16, name="adj_sb")
-        nc.scalar.dma_start(adj_sb[:], adj.rearrange("(nb p) j -> p nb j", p=P))
-        w_sb = held.tile([P, 2, P], BF16, name="w_sb")
-        nc.scalar.dma_start(w_sb[:], w.rearrange("(k c) o -> c k o", c=P))
         windows = [held.tile([P, S], F32, name=f"window{t}") for t in range(T)]
-        for t in range(T):
+        nc.sync.dma_start(windows[0][:], x[0:P, :])
+        w_sb = held.tile([P, 2, P], BF16, name="w_sb")
+        nc.sync.dma_start(w_sb[:], w.rearrange("(k c) o -> c k o", c=P))
+        for t in range(1, T):
             nc.sync.dma_start(windows[t][:], x[t * P : (t + 1) * P, :])
         bias = held.tile([P, 1], F32, name="bias")
         nc.sync.dma_start(bias[:], b)

import concourse.mybir as mybir

F32, BF16, U16 = mybir.dt.float32, mybir.dt.bfloat16, mybir.dt.uint16
ACT = mybir.ActivationFunctionType
ALU = mybir.AluOpType

P = 128
T = 4
S = 512
N = 256
NB = N // P
WARM = 12
WARM_ADJ = 4

FLOPS = T * (2 * P * N * N + 2 * (2 * P) * P * N)
BYTES = 4 * T * P * N + 2 * N * N + 2 * 2 * P * P + 4 * P + 2 * P * (N // 16) + 4 * T * P * N


def tile_adaptivegraphconv_kernel(tc, x, adj, w, b, offs, out):
    nc = tc.nc
    with (
        tc.tile_pool(name="held", bufs=1) as held,
        tc.tile_pool(name="step", bufs=T) as step,
        tc.psum_pool(name="psum", bufs=T) as psum,
        tc.psum_pool(name="psum_mix", bufs=2) as psum_mix,
    ):
        adj_sb = held.tile([P, NB, N], BF16, name="adj_sb")
        nc.sync.dma_start(adj_sb[:], adj.rearrange("(nb p) j -> p nb j", p=P))
        offsets = held.tile([P, N // 16], U16, name="offsets")
        nc.sync.dma_start(offsets[:], offs)
        windows = [held.tile([P, S], F32, name=f"window{t}") for t in range(T)]
        nc.sync.dma_start(windows[0][:], x[0:P, :])
        w_sb = held.tile([P, 2, P], BF16, name="w_sb")
        nc.sync.dma_start(w_sb[:], w.rearrange("(k c) o -> c k o", c=P))
        for t in range(1, T):
            nc.sync.dma_start(windows[t][:], x[t * P : (t + 1) * P, :])
        bias = held.tile([P, 1], F32, name="bias")
        nc.sync.dma_start(bias[:], b)

        ones = held.tile([P, P], BF16, name="ones")
        nc.vector.memset(ones[:], 1.0)
        warm_ps = psum.tile([P, N], F32, name="warm_ps", tag="out_ps")
        for i in range(WARM):
            nc.tensor.matmul(warm_ps[:, 0:P], ones[:], ones[:], start=True, stop=True)

        w_sum = held.tile([P, P], BF16, name="w_sum")
        nc.vector.tensor_add(w_sum[:], w_sb[:, 0, :], w_sb[:, 1, :])
        w1_neg = held.tile([P, P], BF16, name="w1_neg")
        nc.vector.tensor_scalar_mul(w1_neg[:], w_sb[:, 1, :], -1.0)

        deg_col = held.tile([P, NB], F32, name="deg_col")
        nc.vector.tensor_reduce(deg_col[:], adj_sb[:], axis=mybir.AxisListType.X, op=ALU.add)
        deg_row_ps = psum_mix.tile([P, N], F32, name="deg_row_ps", tag="mixed_ps0")
        for nb in range(NB):
            nc.tensor.matmul(deg_row_ps[:], ones[:], adj_sb[:, nb, :], start=(nb == 0), stop=(nb == NB - 1))
        for i in range(WARM_ADJ):
            nc.tensor.matmul(warm_ps[:], ones[:], adj_sb[:, i % NB, :], start=True, stop=True)
        dis_col = held.tile([P, NB], F32, name="dis_col")
        nc.scalar.activation(dis_col[:], deg_col[:], ACT.Abs_reciprocal_sqrt)
        dis_row = held.tile([P, N], F32, name="dis_row")
        nc.scalar.activation(dis_row[:], deg_row_ps[:], ACT.Abs_reciprocal_sqrt)
        adj_hat = held.tile([P, NB, N], BF16, name="adj_hat")
        for nb in range(NB):
            nc.vector.scalar_tensor_tensor(
                adj_hat[:, nb, :], adj_sb[:, nb, :], dis_col[:, nb : nb + 1], dis_row[:], op0=ALU.mult, op1=ALU.mult
            )

        mixeds, out_pss = [], []
        for u in range(T + 1):
            if u < T:
                t = u
                h = step.tile([P, N], F32, name="h")
                nc.scalar.activation(h[:], windows[t][:].indirect(offsets[:]), ACT.Copy)
                h_bf = h[:].bitcast(BF16).rearrange("c (j half) -> c j half", half=2)[:, :, 1]

                mixed = step.tile([P, NB, P], BF16, name="mixed")
                for nb in range(NB):
                    mixed_ps = psum_mix.tile([P, P], BF16, name=f"mixed_ps{nb}")
                    nc.tensor.matmul(mixed_ps[:], h_bf[:, nb * P : (nb + 1) * P], w1_neg[:], start=True, stop=True)
                    nc.vector.tensor_copy(mixed[:, nb, :], mixed_ps[:])
                out_ps = psum.tile([P, N], F32, name="out_ps")
                nc.tensor.matmul(out_ps[:], w_sum[:], h_bf, start=True, stop=False)
                mixeds.append(mixed)
                out_pss.append(out_ps)
            if u >= 1:
                t = u - 1
                for nb in range(NB):
                    nc.tensor.matmul(
                        out_pss[t][:], mixeds[t][:, nb, :], adj_hat[:, nb, :], start=False, stop=(nb == NB - 1)
                    )
                out_sb = step.tile([P, N], F32, name="out_sb")
                for half in range(2):
                    cols = slice(half * (N // 2), (half + 1) * (N // 2))
                    if t % 2 == 0:
                        nc.vector.tensor_scalar_add(out_sb[:, cols], out_pss[t][:, cols], bias[:])
                        nc.sync.dma_start(out[t * P : (t + 1) * P, cols], out_sb[:, cols])
                    else:
                        nc.scalar.activation(out_sb[:, cols], out_pss[t][:, cols], ACT.Identity, bias=bias[:])
                        nc.scalar.dma_start(out[t * P : (t + 1) * P, cols], out_sb[:, cols])
